import numpy as np
import ml_dtypes


def mxq(x, axis, fmt="e4m3"):
    dtype, down = {"e4m3": (ml_dtypes.float8_e4m3fn, 7), "e5m2": (ml_dtypes.float8_e5m2, 14)}[fmt]
    v = np.moveaxis(np.asarray(x, np.float32).astype(ml_dtypes.bfloat16).astype(np.float64), axis, -1)
    blocks = v.reshape(v.shape[:-1] + (-1, 32))
    amax = np.abs(blocks).max(-1, keepdims=True)
    byte = np.maximum(np.where(amax > 0, np.frexp(amax)[1] - 1 + 127, 0) - down, 1)
    scale = np.exp2(byte - 127.0)
    codes = (blocks / scale).astype(np.float32).astype(dtype).astype(np.float64)
    return np.moveaxis((codes * scale).reshape(v.shape), -1, axis)


WIDE = False


def mx_kscale(k):
    if not WIDE:
        return np.ones(k)
    levels = np.array([10, -10, 5, -5, 0])
    a = np.random.permutation(np.resize(levels, k // 512 * 4)).reshape(k // 512, 4)
    idx = np.arange(k)
    return np.exp2(a[idx // 512, idx % 128 // 32])


BF16 = ml_dtypes.bfloat16


def bf(x):
    return np.asarray(x, np.float32).astype(BF16)


def f64(x):
    return np.asarray(x).astype(np.float64)


B, IN_C, OUT_C, HM, HN, NL = 4096, 1024, 512, 32, 16, 3


def leaky(v, leak):
    return np.where(v < 0, v * leak, v)


def setup_inputs():
    s = mx_kscale(IN_C)
    return {"x": bf(np.random.standard_normal((B, IN_C)) * s),
            "W_im": bf(np.random.standard_normal((HN, IN_C, HM)) * 0.7 / np.sqrt(IN_C) / s[None, :, None]),
            "W_in": bf(np.random.standard_normal((HM, IN_C, HN)) * 0.7 / np.sqrt(IN_C) / s[None, :, None]),
            "leak_m": bf(np.random.uniform(-2.0, 2.0, HM)),
            "leak_n": bf(np.random.uniform(-2.0, 2.0, HN))}


def reference(x, W_im, W_in, leak_m, leak_n):
    xq = mxq(f64(x), 1, "e4m3")
    wim = mxq(f64(W_im), 1, "e4m3").transpose(1, 0, 2).reshape(IN_C, HN * HM)
    win = mxq(f64(W_in), 1, "e4m3").transpose(1, 0, 2).reshape(IN_C, HM * HN)
    x_m = leaky((xq @ wim).reshape(B, HN, HM), f64(leak_m))
    x_n = leaky((xq @ win).reshape(B, HM, HN), f64(leak_n))
    return x_m + x_n.transpose(0, 2, 1)

@@ -1,0 +1,260 @@
+from contextlib import ExitStack
+
+import concourse.mybir as mybir
+from concourse.masks import make_identity
+
+FLOPS = 2 * 4096 * 1024 * 1024
+
+F32 = mybir.dt.float32
+BF16 = mybir.dt.bfloat16
+U32 = mybir.dt.uint32
+U8 = mybir.dt.uint8
+FP8X4 = mybir.dt.float8_e4m3fn_x4
+ALU = mybir.AluOpType
+ACT = mybir.ActivationFunctionType
+
+P = 128
+ROWS = 4096
+K = 1024
+HN = 16
+HM = 32
+C = HN * HM
+PACK = 4
+K_PASS = P * PACK
+PASSES = K // K_PASS
+TILES = ROWS // P
+GT = 4
+GROUPS = TILES // GT
+NB = C // P
+
+
+def tile_tensormoe_pa_t_kernel(tc, x, W_im, W_in, leak_m, leak_n, out):
+    nc = tc.nc
+    xv = x.rearrange("(p t) k -> p t k", t=TILES)
+    ov = out.rearrange("(p t) n m -> p t (n m)", t=TILES)
+
+    with ExitStack() as ctx:
+        const = ctx.enter_context(tc.tile_pool(name="const", bufs=1))
+        xpool = ctx.enter_context(tc.tile_pool(name="xpool", bufs=4))
+        grpool = ctx.enter_context(tc.tile_pool(name="grpool", bufs=4))
+        work = ctx.enter_context(tc.tile_pool(name="work", bufs=3))
+        ypool = ctx.enter_context(tc.tile_pool(name="ypool", bufs=3))
+        psx = ctx.enter_context(tc.psum_pool(name="psx", bufs=4))
+        psa = ctx.enter_context(tc.psum_pool(name="psa", bufs=2))
+        psb = ctx.enter_context(tc.psum_pool(name="psb", bufs=2))
+
+        ident = const.tile([P, P], F32, name="ident")
+        make_identity(nc, ident[:])
+        lm_bf = const.tile([P, HM], BF16, name="lm_bf")
+        ln_bf = const.tile([P, HN], BF16, name="ln_bf")
+        nc.scalar.dma_start(out=lm_bf[:], in_=leak_m.partition_broadcast(P))
+        nc.scalar.dma_start(out=ln_bf[:], in_=leak_n.partition_broadcast(P))
+
+        xq = const.tile([P, TILES, PASSES * P], U32, name="xq", align_bytes=64)
+        xs = const.tile([P, TILES, PASSES * P], U8, name="xs", align_bytes=64)
+        raw_im = const.tile([P, PASSES, HN, PACK * HM], BF16, name="raw_im")
+        raw_in = const.tile([P, PASSES, HM, PACK * HN], BF16, name="raw_in")
+        grp_im = const.tile([P, PASSES, C, PACK], BF16, name="grp_im", align_bytes=64)
+        grp_in = const.tile([P, PASSES, C, PACK], BF16, name="grp_in", align_bytes=64)
+        wq_im = const.tile([P, PASSES, C], U32, name="wq_im", align_bytes=64)
+        wq_in = const.tile([P, PASSES, C], U32, name="wq_in", align_bytes=64)
+        ws_im = const.tile([P, PASSES, C], U8, name="ws_im", align_bytes=64)
+        ws_in = const.tile([P, PASSES, C], U8, name="ws_in", align_bytes=64)
+        lm1 = const.tile([P, HN, HM], F32, name="lm1")
+        dn = const.tile([P, HN], F32, name="dn")
+
+        x_tiles = {}
+        xt_tiles = {}
+        gr_tiles = {}
+        a_tiles = {}
+        b_tiles = {}
+        rb_tiles = {}
+        y1_tiles = {}
+        y2_tiles = {}
+
+        def load_x(gi, pieces):
+            x_sb = xpool.tile([P, GT, K], BF16, name="x_sb")
+            x_tiles[gi] = x_sb
+            step = GT // pieces
+            for h in range(pieces):
+                nc.sync.dma_start(
+                    out=x_sb[:, h * step : (h + 1) * step, :],
+                    in_=xv[:, gi * GT + h * step : gi * GT + (h + 1) * step, :],
+                )
+
+        def load_w_im(g):
+            nc.sync.dma_start(
+                out=raw_im[:, g],
+                in_=W_im[:, g * K_PASS : (g + 1) * K_PASS, :].rearrange("n (p j) m -> p n (j m)", j=PACK),
+            )
+
+        def load_w_in(g):
+            nc.sync.dma_start(
+                out=raw_in[:, g],
+                in_=W_in[:, g * K_PASS : (g + 1) * K_PASS, :].rearrange("m (p j) n -> p m (j n)", j=PACK),
+            )
+
+        def regroup_im(g):
+            nc.vector.tensor_copy(
+                out=grp_im[:, g].rearrange("p (n m) j -> p n m j", n=HN),
+                in_=raw_im[:, g].rearrange("p n (j m) -> p n m j", j=PACK),
+            )
+
+        def regroup_in(g):
+            nc.scalar.copy(
+                out=grp_in[:, g].rearrange("p (n m) j -> p n m j", n=HN),
+                in_=raw_in[:, g].rearrange("p m (j n) -> p n m j", j=PACK),
+            )
+
+        def quant_w(grp, wq, ws, g):
+            nc.vector.quantize_mx(
+                out=wq[:, g, :].bitcast(FP8X4),
+                scales=ws[:, g, :],
+                in_=grp[:, g].rearrange("p c j -> p (c j)"),
+            )
+
+        def transposes(gi):
+            for tt in range(GT):
+                xw = x_tiles[gi][:, tt, :].bitcast(F32)
+                xt = psx.tile([P, PACK, P], F32, name="xt")
+                xt_tiles[(gi, tt)] = xt
+                for q in range(PACK):
+                    g, u = divmod(q, 2)
+                    nc.tensor.transpose(
+                        xt[:, q, :], xw[:, 256 * g + u : 256 * (g + 1) : 2], ident[:]
+                    )
+
+        def evac(gi, tt):
+            gr = grpool.tile([P, PASSES, P, 2], F32, name="gr", align_bytes=64)
+            gr_tiles[(gi, tt)] = gr
+            nc.scalar.copy(
+                out=gr[:], in_=xt_tiles[(gi, tt)][:].rearrange("p (g u) b -> p g b u", u=2)
+            )
+
+        def quant_x(gi, tt):
+            t = gi * GT + tt
+            nc.vector.quantize_mx(
+                out=xq[:, t, :].bitcast(FP8X4),
+                scales=xs[:, t, :],
+                in_=gr_tiles[(gi, tt)][:].rearrange("p g b u -> p (g b u)").bitcast(BF16),
+            )
+
+        def mx(acc, t, g, wq, ws, cols):
+            nc.tensor.matmul_mx(
+                out=acc,
+                lhsT=xq[:, t, g * P : (g + 1) * P].bitcast(FP8X4),
+                lhsT_scale=xs[:, t, g * P : (g + 1) * P],
+                rhs=wq[:, g, cols].bitcast(FP8X4),
+                rhs_scale=ws[:, g, cols],
+                start=(g == 0),
+                stop=(g == PASSES - 1),
+            )
+
+        def a_passes(gi, tt):
+            a_ps = psa.tile([P, C], F32, name="a_ps")
+            a_tiles[(gi, tt)] = a_ps
+            for g in range(PASSES):
+                mx(a_ps[:], gi * GT + tt, g, wq_im, ws_im, slice(0, C))
+
+        def b_passes(gi, j):
+            b_ps = psb.tile([P, GT, P], F32, name="b_ps")
+            b_tiles[(gi, j)] = b_ps
+            for tt in range(GT):
+                for g in range(PASSES):
+                    mx(b_ps[:, tt, :], gi * GT + tt, g, wq_in, ws_in, slice(j * P, (j + 1) * P))
+
+        def a_elem(gi, tt):
+            if tt == 0:
+                y1 = ypool.tile([P, GT, C], F32, name="y1")
+                y1_tiles[gi] = y1
+            a_ps = a_tiles[(gi, tt)]
+            t1 = work.tile([P, C], F32, name="t1")
+            nc.vector.scalar_tensor_tensor(
+                out=t1[:], in0=a_ps[:], scalar=0.0, in1=lm1[:].rearrange("p n m -> p (n m)"),
+                op0=ALU.min, op1=ALU.mult,
+            )
+            nc.vector.tensor_tensor(out=y1_tiles[gi][:, tt, :], in0=a_ps[:], in1=t1[:], op=ALU.add)
+
+        def b_relu(gi, j):
+            rb = work.tile([P, GT, P], F32, name="rb")
+            rb_tiles[(gi, j)] = rb
+            nc.scalar.activation(out=rb[:], in_=b_tiles[(gi, j)][:], func=ACT.Relu, scale=-1.0)
+
+        def b_elem(gi, j):
+            if j == 0:
+                y2 = ypool.tile([P, GT, C], F32, name="y2")
+                y2_tiles[gi] = y2
+            y2 = y2_tiles[gi]
+            for nl in range(P // HM):
+                n = j * (P // HM) + nl
+                nc.vector.scalar_tensor_tensor(
+                    out=y2[:, :, n * HM : (n + 1) * HM],
+                    in0=rb_tiles[(gi, j)][:, :, nl * HM : (nl + 1) * HM],
+                    scalar=dn[:, n : n + 1],
+                    in1=b_tiles[(gi, j)][:, :, nl * HM : (nl + 1) * HM],
+                    op0=ALU.mult, op1=ALU.add,
+                )
+
+        def final_add(gi, j):
+            cols = slice(j * P, (j + 1) * P)
+            nc.gpsimd.tensor_tensor(
+                out=y2_tiles[gi][:, :, cols], in0=y1_tiles[gi][:, :, cols],
+                in1=y2_tiles[gi][:, :, cols], op=ALU.add,
+            )
+
+        def store(gi):
+            nc.sync.dma_start(out=ov[:, gi * GT : (gi + 1) * GT, :], in_=y2_tiles[gi][:])
+
+        load_x(0, 2)
+        load_w_im(0)
+        load_w_im(1)
+        load_x(1, 1)
+        load_w_in(0)
+        load_w_in(1)
+        load_x(2, 1)
+        load_x(3, 1)
+
+        for it in range(-2, GROUPS):
+            gx, ga, gb = it + 2, it + 1, it
+            do_x = gx < GROUPS
+            do_a = 0 <= ga < GROUPS
+            do_b = gb >= 0
+            if do_x:
+                transposes(gx)
+                if gx + 4 < GROUPS:
+                    load_x(gx + 4, 1)
+            for s in range(GT):
+                if do_b:
+                    b_passes(gb, s)
+                if do_a:
+                    a_passes(ga, s)
+                if do_b:
+                    b_relu(gb, s)
+                if do_x:
+                    evac(gx, s)
+                if do_b:
+                    b_elem(gb, s)
+                    final_add(gb, s)
+                if do_a:
+                    a_elem(ga, s)
+                if do_x:
+                    quant_x(gx, s)
+                if it == -2 and s % 2 == 1:
+                    regroup_im(s // 2)
+                if it == -1 and s % 2 == 1:
+                    regroup_in(s // 2)
+            if it == -2:
+                quant_w(grp_im, wq_im, ws_im, 0)
+                quant_w(grp_im, wq_im, ws_im, 1)
+                nc.vector.tensor_scalar(
+                    out=lm1[:], in0=lm_bf[:].unsqueeze(1).to_broadcast([P, HN, HM]),
+                    scalar1=-1.0, scalar2=None, op0=ALU.add,
+                )
+                nc.vector.tensor_scalar(
+                    out=dn[:], in0=ln_bf[:], scalar1=-1.0, scalar2=1.0, op0=ALU.mult, op1=ALU.add,
+                )
+            if it == -1:
+                quant_w(grp_in, wq_in, ws_in, 0)
+                quant_w(grp_in, wq_in, ws_in, 1)
+            if do_b:
+                store(gb)

@@ -26,6 +26,8 @@ TILES = ROWS // P
 GT = 4
 GROUPS = TILES // GT
 NB = C // P
+LAG_A = 2
+LAG_X = 3
 
 
 def tile_tensormoe_pa_t_kernel(tc, x, W_im, W_in, leak_m, leak_n, out):
@@ -36,12 +38,14 @@ def tile_tensormoe_pa_t_kernel(tc, x, W_im, W_in, leak_m, leak_n, out):
     with ExitStack() as ctx:
         const = ctx.enter_context(tc.tile_pool(name="const", bufs=1))
         xpool = ctx.enter_context(tc.tile_pool(name="xpool", bufs=4))
-        grpool = ctx.enter_context(tc.tile_pool(name="grpool", bufs=4))
+        grpool = ctx.enter_context(tc.tile_pool(name="grpool", bufs=3))
         work = ctx.enter_context(tc.tile_pool(name="work", bufs=3))
-        ypool = ctx.enter_context(tc.tile_pool(name="ypool", bufs=3))
-        psx = ctx.enter_context(tc.psum_pool(name="psx", bufs=4))
-        psa = ctx.enter_context(tc.psum_pool(name="psa", bufs=2))
-        psb = ctx.enter_context(tc.psum_pool(name="psb", bufs=2))
+        y1pool = ctx.enter_context(tc.tile_pool(name="y1pool", bufs=4))
+        y2pool = ctx.enter_context(tc.tile_pool(name="y2pool", bufs=3))
+        psx = ctx.enter_context(tc.psum_pool(name="psx", bufs=2))
+        psa = ctx.enter_context(tc.psum_pool(name="psa", bufs=3))
+        psb = ctx.enter_context(tc.psum_pool(name="psb", bufs=3))
+        ctx.enter_context(tc.manual_schedule())
 
         ident = const.tile([P, P], F32, name="ident")
         make_identity(nc, ident[:])
@@ -67,6 +71,7 @@ def tile_tensormoe_pa_t_kernel(tc, x, W_im, W_in, leak_m, leak_n, out):
         xt_tiles = {}
         gr_tiles = {}
         a_tiles = {}
+        t1_tiles = {}
         b_tiles = {}
         rb_tiles = {}
         y1_tiles = {}
@@ -101,9 +106,10 @@ def tile_tensormoe_pa_t_kernel(tc, x, W_im, W_in, leak_m, leak_n, out):
             )
 
         def regroup_in(g):
-            nc.scalar.copy(
+            nc.gpsimd.tensor_scalar(
                 out=grp_in[:, g].rearrange("p (n m) j -> p n m j", n=HN),
-                in_=raw_in[:, g].rearrange("p m (j n) -> p n m j", j=PACK),
+                in0=raw_in[:, g].rearrange("p m (j n) -> p n m j", j=PACK),
+                scalar1=1.0, scalar2=0.0, op0=ALU.mult, op1=ALU.add,
             )
 
         def quant_w(grp, wq, ws, g):
@@ -113,8 +119,8 @@ def tile_tensormoe_pa_t_kernel(tc, x, W_im, W_in, leak_m, leak_n, out):
                 in_=grp[:, g].rearrange("p c j -> p (c j)"),
             )
 
-        def transposes(gi):
-            for tt in range(GT):
+        def transposes(gi, h):
+            for tt in (2 * h, 2 * h + 1):
                 xw = x_tiles[gi][:, tt, :].bitcast(F32)
                 xt = psx.tile([P, PACK, P], F32, name="xt")
                 xt_tiles[(gi, tt)] = xt
@@ -124,19 +130,21 @@ def tile_tensormoe_pa_t_kernel(tc, x, W_im, W_in, leak_m, leak_n, out):
                         xt[:, q, :], xw[:, 256 * g + u : 256 * (g + 1) : 2], ident[:]
                     )
 
-        def evac(gi, tt):
-            gr = grpool.tile([P, PASSES, P, 2], F32, name="gr", align_bytes=64)
-            gr_tiles[(gi, tt)] = gr
-            nc.scalar.copy(
-                out=gr[:], in_=xt_tiles[(gi, tt)][:].rearrange("p (g u) b -> p g b u", u=2)
-            )
+        def evac(gi, h):
+            gr = grpool.tile([P, 2, PASSES, P, 2], F32, name="gr", align_bytes=64)
+            gr_tiles[(gi, h)] = gr
+            for e in range(2):
+                nc.scalar.copy(
+                    out=gr[:, e],
+                    in_=xt_tiles[(gi, 2 * h + e)][:].rearrange("p (g u) b -> p g b u", u=2),
+                )
 
-        def quant_x(gi, tt):
-            t = gi * GT + tt
+        def quant_x(gi, h):
+            t = gi * GT + 2 * h
             nc.vector.quantize_mx(
-                out=xq[:, t, :].bitcast(FP8X4),
-                scales=xs[:, t, :],
-                in_=gr_tiles[(gi, tt)][:].rearrange("p g b u -> p (g b u)").bitcast(BF16),
+                out=xq[:, t : t + 2, :].rearrange("p t w -> p (t w)").bitcast(FP8X4),
+                scales=xs[:, t : t + 2, :].rearrange("p t w -> p (t w)"),
+                in_=gr_tiles[(gi, h)][:].rearrange("p e g b u -> p (e g b u)").bitcast(BF16),
             )
 
         def mx(acc, t, g, wq, ws, cols):
@@ -163,17 +171,22 @@ def tile_tensormoe_pa_t_kernel(tc, x, W_im, W_in, leak_m, leak_n, out):
                 for g in range(PASSES):
                     mx(b_ps[:, tt, :], gi * GT + tt, g, wq_in, ws_in, slice(j * P, (j + 1) * P))
 
-        def a_elem(gi, tt):
-            if tt == 0:
-                y1 = ypool.tile([P, GT, C], F32, name="y1")
-                y1_tiles[gi] = y1
-            a_ps = a_tiles[(gi, tt)]
+        def a_mul(gi, tt):
             t1 = work.tile([P, C], F32, name="t1")
+            t1_tiles[(gi, tt)] = t1
             nc.vector.scalar_tensor_tensor(
-                out=t1[:], in0=a_ps[:], scalar=0.0, in1=lm1[:].rearrange("p n m -> p (n m)"),
-                op0=ALU.min, op1=ALU.mult,
+                out=t1[:], in0=a_tiles[(gi, tt)][:], scalar=0.0,
+                in1=lm1[:].rearrange("p n m -> p (n m)"), op0=ALU.min, op1=ALU.mult,
             )
-            nc.vector.tensor_tensor(out=y1_tiles[gi][:, tt, :], in0=a_ps[:], in1=t1[:], op=ALU.add)
+
+        def a_add(gi, tt):
+            if tt == 0:
+                y1 = y1pool.tile([P, GT, C], F32, name="y1")
+                y1_tiles[gi] = y1
+            nc.vector.tensor_tensor(
+                out=y1_tiles[gi][:, tt, :], in0=a_tiles[(gi, tt)][:], in1=t1_tiles[(gi, tt)][:],
+                op=ALU.add,
+            )
 
         def b_relu(gi, j):
             rb = work.tile([P, GT, P], F32, name="rb")
@@ -182,7 +195,7 @@ def tile_tensormoe_pa_t_kernel(tc, x, W_im, W_in, leak_m, leak_n, out):
 
         def b_elem(gi, j):
             if j == 0:
-                y2 = ypool.tile([P, GT, C], F32, name="y2")
+                y2 = y2pool.tile([P, GT, C], F32, name="y2")
                 y2_tiles[gi] = y2
             y2 = y2_tiles[gi]
             for nl in range(P // HM):
@@ -195,66 +208,75 @@ def tile_tensormoe_pa_t_kernel(tc, x, W_im, W_in, leak_m, leak_n, out):
                     op0=ALU.mult, op1=ALU.add,
                 )
 
-        def final_add(gi, j):
+        def final_add(eng, gi, j):
             cols = slice(j * P, (j + 1) * P)
-            nc.gpsimd.tensor_tensor(
+            eng.tensor_tensor(
                 out=y2_tiles[gi][:, :, cols], in0=y1_tiles[gi][:, :, cols],
                 in1=y2_tiles[gi][:, :, cols], op=ALU.add,
             )
-
-        def store(gi):
-            nc.sync.dma_start(out=ov[:, gi * GT : (gi + 1) * GT, :], in_=y2_tiles[gi][:])
 
         load_x(0, 2)
         load_w_im(0)
         load_w_im(1)
         load_x(1, 1)
+        load_x(2, 1)
         load_w_in(0)
         load_w_in(1)
-        load_x(2, 1)
         load_x(3, 1)
 
-        for it in range(-2, GROUPS):
-            gx, ga, gb = it + 2, it + 1, it
+        nc.vector.tensor_scalar(
+            out=lm1[:], in0=lm_bf[:].unsqueeze(1).to_broadcast([P, HN, HM]),
+            scalar1=-1.0, scalar2=None, op0=ALU.add,
+        )
+        nc.vector.tensor_scalar(
+            out=dn[:], in0=ln_bf[:], scalar1=-1.0, scalar2=1.0, op0=ALU.mult, op1=ALU.add,
+        )
+
+        for gb in range(-LAG_X, GROUPS):
+            ga = gb + LAG_A
+            gx = gb + LAG_X
             do_x = gx < GROUPS
             do_a = 0 <= ga < GROUPS
             do_b = gb >= 0
-            if do_x:
-                transposes(gx)
-                if gx + 4 < GROUPS:
-                    load_x(gx + 4, 1)
             for s in range(GT):
-                if do_b:
-                    b_passes(gb, s)
                 if do_a:
                     a_passes(ga, s)
                 if do_b:
+                    b_passes(gb, s)
+                if do_x and s % 2 == 0:
+                    transposes(gx, s // 2)
+                    if s == 2 and gx + 4 < GROUPS:
+                        load_x(gx + 4, 1)
+                if do_x and s % 2 == 1:
+                    evac(gx, s // 2)
+                if do_b:
                     b_relu(gb, s)
-                if do_x:
-                    evac(gx, s)
+                if do_a:
+                    a_mul(ga, s)
+                if do_x and s >= 2:
+                    quant_x(gx, s - 2)
+                if gx == 0 and s >= 2:
+                    regroup_im(s - 2)
+                if gx == 0 and s == 3:
+                    quant_w(grp_im, wq_im, ws_im, 0)
+                    quant_w(grp_im, wq_im, ws_im, 1)
+                if gx == 1 and s >= 2:
+                    regroup_in(s - 2)
+                if gx == 2 and s >= 2:
+                    quant_w(grp_in, wq_in, ws_in, s - 2)
                 if do_b:
                     b_elem(gb, s)
-                    final_add(gb, s)
                 if do_a:
-                    a_elem(ga, s)
-                if do_x:
-                    quant_x(gx, s)
-                if it == -2 and s % 2 == 1:
-                    regroup_im(s // 2)
-                if it == -1 and s % 2 == 1:
-                    regroup_in(s // 2)
-            if it == -2:
-                quant_w(grp_im, wq_im, ws_im, 0)
-                quant_w(grp_im, wq_im, ws_im, 1)
-                nc.vector.tensor_scalar(
-                    out=lm1[:], in0=lm_bf[:].unsqueeze(1).to_broadcast([P, HN, HM]),
-                    scalar1=-1.0, scalar2=None, op0=ALU.add,
-                )
-                nc.vector.tensor_scalar(
-                    out=dn[:], in0=ln_bf[:], scalar1=-1.0, scalar2=1.0, op0=ALU.mult, op1=ALU.add,
-                )
-            if it == -1:
-                quant_w(grp_in, wq_in, ws_in, 0)
-                quant_w(grp_in, wq_in, ws_in, 1)
-            if do_b:
-                store(gb)
+                    a_add(ga, s)
+                if do_b:
+                    if not do_a and s % 2 == 0:
+                        final_add(nc.vector, gb, s)
+                    else:
+                        final_add(nc.gpsimd, gb, s)
+                    if gb == GROUPS - 1:
+                        cols = slice(s * P, (s + 1) * P)
+                        nc.sync.dma_start(
+                            out=ov[:, gb * GT : (gb + 1) * GT, cols], in_=y2_tiles[gb][:, :, cols]
+                        )
+            if do_b and gb < GROUPS - 1:
+                nc.sync.dma_start(out=ov[:, gb * GT : (gb + 1) * GT, :], in_=y2_tiles[gb][:])

@@ -193,12 +193,12 @@ def tile_tensormoe_pa_t_kernel(tc, x, W_im, W_in, leak_m, leak_n, out):
             rb_tiles[(gi, j)] = rb
             nc.scalar.activation(out=rb[:], in_=b_tiles[(gi, j)][:], func=ACT.Relu, scale=-1.0)
 
-        def b_elem(gi, j):
-            if j == 0:
+        def b_elem(gi, j, slices):
+            if j == 0 and slices[0] == 0:
                 y2 = y2pool.tile([P, GT, C], F32, name="y2")
                 y2_tiles[gi] = y2
             y2 = y2_tiles[gi]
-            for nl in range(P // HM):
+            for nl in slices:
                 n = j * (P // HM) + nl
                 nc.vector.scalar_tensor_tensor(
                     out=y2[:, :, n * HM : (n + 1) * HM],
@@ -253,6 +253,8 @@ def tile_tensormoe_pa_t_kernel(tc, x, W_im, W_in, leak_m, leak_n, out):
                     b_relu(gb, s)
                 if do_a:
                     a_mul(ga, s)
+                if do_b:
+                    b_elem(gb, s, (0, 1, 2))
                 if do_x and s >= 2:
                     quant_x(gx, s - 2)
                 if gx == 0 and s >= 2:
@@ -265,7 +267,7 @@ def tile_tensormoe_pa_t_kernel(tc, x, W_im, W_in, leak_m, leak_n, out):
                 if gx == 2 and s >= 2:
                     quant_w(grp_in, wq_in, ws_in, s - 2)
                 if do_b:
-                    b_elem(gb, s)
+                    b_elem(gb, s, (3,))
                 if do_a:
                     a_add(ga, s)
                 if do_b:

@@ -28,6 +28,7 @@ GROUPS = TILES // GT
 NB = C // P
 LAG_A = 2
 LAG_X = 3
+N_SPLIT = 11
 
 
 def tile_tensormoe_pa_t_kernel(tc, x, W_im, W_in, leak_m, leak_n, out):
@@ -77,6 +78,12 @@ def tile_tensormoe_pa_t_kernel(tc, x, W_im, W_in, leak_m, leak_n, out):
         y1_tiles = {}
         y2_tiles = {}
 
+        def load_w_im(g):
+            nc.sync.dma_start(
+                out=raw_im[:, g],
+                in_=W_im[:, g * K_PASS : (g + 1) * K_PASS, :].rearrange("n (p j) m -> p n (j m)", j=PACK),
+            )
+
         def load_x(gi, pieces):
             x_sb = xpool.tile([P, GT, K], BF16, name="x_sb")
             x_tiles[gi] = x_sb
@@ -86,12 +93,9 @@ def tile_tensormoe_pa_t_kernel(tc, x, W_im, W_in, leak_m, leak_n, out):
                     out=x_sb[:, h * step : (h + 1) * step, :],
                     in_=xv[:, gi * GT + h * step : gi * GT + (h + 1) * step, :],
                 )
-
-        def load_w_im(g):
-            nc.sync.dma_start(
-                out=raw_im[:, g],
-                in_=W_im[:, g * K_PASS : (g + 1) * K_PASS, :].rearrange("n (p j) m -> p n (j m)", j=PACK),
-            )
+                if gi == 0 and h == 0:
+                    load_w_im(0)
+                    load_w_im(1)
 
         def load_w_in(g):
             nc.sync.dma_start(
@@ -100,10 +104,10 @@ def tile_tensormoe_pa_t_kernel(tc, x, W_im, W_in, leak_m, leak_n, out):
             )
 
         def regroup_im(g):
-            nc.vector.tensor_copy(
-                out=grp_im[:, g].rearrange("p (n m) j -> p n m j", n=HN),
-                in_=raw_im[:, g].rearrange("p n (j m) -> p n m j", j=PACK),
-            )
+            dst = grp_im[:, g].rearrange("p (n m) j -> p n m j", n=HN)
+            src = raw_im[:, g].rearrange("p n (j m) -> p n m j", j=PACK)
+            nc.vector.tensor_copy(out=dst[:, :N_SPLIT], in_=src[:, :N_SPLIT])
+            nc.scalar.copy(out=dst[:, N_SPLIT:], in_=src[:, N_SPLIT:])
 
         def regroup_in(g):
             nc.gpsimd.tensor_scalar(
@@ -216,8 +220,6 @@ def tile_tensormoe_pa_t_kernel(tc, x, W_im, W_in, leak_m, leak_n, out):
             )
 
         load_x(0, 2)
-        load_w_im(0)
-        load_w_im(1)
         load_x(1, 1)
         load_x(2, 1)
         load_w_in(0)
@@ -232,6 +234,7 @@ def tile_tensormoe_pa_t_kernel(tc, x, W_im, W_in, leak_m, leak_n, out):
             out=dn[:], in0=ln_bf[:], scalar1=-1.0, scalar2=1.0, op0=ALU.mult, op1=ALU.add,
         )
 
+        pending_add = []
         for gb in range(-LAG_X, GROUPS):
             ga = gb + LAG_A
             gx = gb + LAG_X
@@ -239,6 +242,8 @@ def tile_tensormoe_pa_t_kernel(tc, x, W_im, W_in, leak_m, leak_n, out):
             do_a = 0 <= ga < GROUPS
             do_b = gb >= 0
             for s in range(GT):
+                if gx == 0 and s >= 2:
+                    regroup_im(s - 2)
                 if do_a:
                     a_passes(ga, s)
                 if do_b:
@@ -255,21 +260,23 @@ def tile_tensormoe_pa_t_kernel(tc, x, W_im, W_in, leak_m, leak_n, out):
                     a_mul(ga, s)
                 if do_b:
                     b_elem(gb, s, (0, 1, 2))
-                if do_x and s >= 2:
-                    quant_x(gx, s - 2)
+                if do_x and s == 2:
+                    quant_x(gx, 0)
+                if 0 < gx <= GROUPS and s == 0:
+                    quant_x(gx - 1, 1)
                 if gx == 0 and s >= 2:
-                    regroup_im(s - 2)
-                if gx == 0 and s == 3:
-                    quant_w(grp_im, wq_im, ws_im, 0)
-                    quant_w(grp_im, wq_im, ws_im, 1)
+                    quant_w(grp_im, wq_im, ws_im, s - 2)
                 if gx == 1 and s >= 2:
                     regroup_in(s - 2)
                 if gx == 2 and s >= 2:
                     quant_w(grp_in, wq_in, ws_in, s - 2)
                 if do_b:
                     b_elem(gb, s, (3,))
+                for item in pending_add:
+                    a_add(item[0], item[1])
+                pending_add = []
                 if do_a:
-                    a_add(ga, s)
+                    pending_add.append((ga, s))
                 if do_b:
                     if not do_a and s % 2 == 0:
                         final_add(nc.vector, gb, s)

@@ -45,7 +45,8 @@ def tile_tensormoe_pa_t_kernel(tc, x, W_im, W_in, leak_m, leak_n, out):
         y2pool = ctx.enter_context(tc.tile_pool(name="y2pool", bufs=3))
         psx = ctx.enter_context(tc.psum_pool(name="psx", bufs=2))
         psa = ctx.enter_context(tc.psum_pool(name="psa", bufs=3))
-        psb = ctx.enter_context(tc.psum_pool(name="psb", bufs=3))
+        psb = ctx.enter_context(tc.psum_pool(name="psb", bufs=2))
+        psp = ctx.enter_context(tc.psum_pool(name="psp", bufs=1))
         ctx.enter_context(tc.manual_schedule())
 
         ident = const.tile([P, P], F32, name="ident")
@@ -66,7 +67,9 @@ def tile_tensormoe_pa_t_kernel(tc, x, W_im, W_in, leak_m, leak_n, out):
         ws_im = const.tile([P, PASSES, C], U8, name="ws_im", align_bytes=64)
         ws_in = const.tile([P, PASSES, C], U8, name="ws_in", align_bytes=64)
         lm1 = const.tile([P, HN, HM], F32, name="lm1")
-        dn = const.tile([P, HN], F32, name="dn")
+        dn_sb = const.tile([P, P], F32, name="dn_sb")
+        dn_t = const.tile([P, P], F32, name="dn_t")
+        dn = psp.tile([P, P], F32, name="dn")
 
         x_tiles = {}
         xt_tiles = {}
@@ -230,11 +233,11 @@ def tile_tensormoe_pa_t_kernel(tc, x, W_im, W_in, leak_m, leak_n, out):
             out=lm1[:], in0=lm_bf[:].unsqueeze(1).to_broadcast([P, HN, HM]),
             scalar1=-1.0, scalar2=None, op0=ALU.add,
         )
+        nc.vector.memset(dn_sb[:], 0.0)
         nc.vector.tensor_scalar(
-            out=dn[:], in0=ln_bf[:], scalar1=-1.0, scalar2=1.0, op0=ALU.mult, op1=ALU.add,
+            out=dn_sb[:, :HN], in0=ln_bf[:], scalar1=-1.0, scalar2=1.0, op0=ALU.mult, op1=ALU.add,
         )
 
-        pending_add = []
         for gb in range(-LAG_X, GROUPS):
             ga = gb + LAG_A
             gx = gb + LAG_X
@@ -252,12 +255,19 @@ def tile_tensormoe_pa_t_kernel(tc, x, W_im, W_in, leak_m, leak_n, out):
                     transposes(gx, s // 2)
                     if s == 2 and gx + 4 < GROUPS:
                         load_x(gx + 4, 1)
+                if gx == 0 and s == 3:
+                    dn_ps = psx.tile([P, PACK, P], F32, name="xt")
+                    nc.tensor.transpose(dn_ps[:, 0, :], dn_sb[:], ident[:])
+                if gx == 1 and s == 1:
+                    nc.tensor.transpose(dn[:], dn_t[:], ident[:])
                 if do_x and s % 2 == 1:
                     evac(gx, s // 2)
                 if do_b:
                     b_relu(gb, s)
                 if do_a:
                     a_mul(ga, s)
+                if gx == 1 and s == 0:
+                    nc.vector.tensor_copy(out=dn_t[:], in_=dn_ps[:, 0, :])
                 if do_b:
                     b_elem(gb, s, (0, 1, 2))
                 if do_x and s == 2:
@@ -272,11 +282,8 @@ def tile_tensormoe_pa_t_kernel(tc, x, W_im, W_in, leak_m, leak_n, out):
                     quant_w(grp_in, wq_in, ws_in, s - 2)
                 if do_b:
                     b_elem(gb, s, (3,))
-                for item in pending_add:
-                    a_add(item[0], item[1])
-                pending_add = []
                 if do_a:
-                    pending_add.append((ga, s))
+                    a_add(ga, s)
                 if do_b:
                     if not do_a and s % 2 == 0:
                         final_add(nc.vector, gb, s)

@@ -45,8 +45,7 @@ def tile_tensormoe_pa_t_kernel(tc, x, W_im, W_in, leak_m, leak_n, out):
         y2pool = ctx.enter_context(tc.tile_pool(name="y2pool", bufs=3))
         psx = ctx.enter_context(tc.psum_pool(name="psx", bufs=2))
         psa = ctx.enter_context(tc.psum_pool(name="psa", bufs=3))
-        psb = ctx.enter_context(tc.psum_pool(name="psb", bufs=2))
-        psp = ctx.enter_context(tc.psum_pool(name="psp", bufs=1))
+        psb = ctx.enter_context(tc.psum_pool(name="psb", bufs=3))
         ctx.enter_context(tc.manual_schedule())
 
         ident = const.tile([P, P], F32, name="ident")
@@ -67,9 +66,7 @@ def tile_tensormoe_pa_t_kernel(tc, x, W_im, W_in, leak_m, leak_n, out):
         ws_im = const.tile([P, PASSES, C], U8, name="ws_im", align_bytes=64)
         ws_in = const.tile([P, PASSES, C], U8, name="ws_in", align_bytes=64)
         lm1 = const.tile([P, HN, HM], F32, name="lm1")
-        dn_sb = const.tile([P, P], F32, name="dn_sb")
-        dn_t = const.tile([P, P], F32, name="dn_t")
-        dn = psp.tile([P, P], F32, name="dn")
+        dn = const.tile([P, HN], F32, name="dn")
 
         x_tiles = {}
         xt_tiles = {}
@@ -233,9 +230,8 @@ def tile_tensormoe_pa_t_kernel(tc, x, W_im, W_in, leak_m, leak_n, out):
             out=lm1[:], in0=lm_bf[:].unsqueeze(1).to_broadcast([P, HN, HM]),
             scalar1=-1.0, scalar2=None, op0=ALU.add,
         )
-        nc.vector.memset(dn_sb[:], 0.0)
         nc.vector.tensor_scalar(
-            out=dn_sb[:, :HN], in0=ln_bf[:], scalar1=-1.0, scalar2=1.0, op0=ALU.mult, op1=ALU.add,
+            out=dn[:], in0=ln_bf[:], scalar1=-1.0, scalar2=1.0, op0=ALU.mult, op1=ALU.add,
         )
 
         for gb in range(-LAG_X, GROUPS):
@@ -255,19 +251,12 @@ def tile_tensormoe_pa_t_kernel(tc, x, W_im, W_in, leak_m, leak_n, out):
                     transposes(gx, s // 2)
                     if s == 2 and gx + 4 < GROUPS:
                         load_x(gx + 4, 1)
-                if gx == 0 and s == 3:
-                    dn_ps = psx.tile([P, PACK, P], F32, name="xt")
-                    nc.tensor.transpose(dn_ps[:, 0, :], dn_sb[:], ident[:])
-                if gx == 1 and s == 1:
-                    nc.tensor.transpose(dn[:], dn_t[:], ident[:])
                 if do_x and s % 2 == 1:
                     evac(gx, s // 2)
                 if do_b:
                     b_relu(gb, s)
                 if do_a:
                     a_mul(ga, s)
-                if gx == 1 and s == 0:
-                    nc.vector.tensor_copy(out=dn_t[:], in_=dn_ps[:, 0, :])
                 if do_b:
                     b_elem(gb, s, (0, 1, 2))
                 if do_x and s == 2:

@@ -28,7 +28,7 @@ GROUPS = TILES // GT
 NB = C // P
 LAG_A = 2
 LAG_X = 3
-N_SPLIT = 11
+N_SPLIT = 10
 
 
 def tile_tensormoe_pa_t_kernel(tc, x, W_im, W_in, leak_m, leak_n, out):
@@ -274,7 +274,7 @@ def tile_tensormoe_pa_t_kernel(tc, x, W_im, W_in, leak_m, leak_n, out):
                 if do_a:
                     a_add(ga, s)
                 if do_b:
-                    if not do_a and s % 2 == 0:
+                    if (not do_a and s % 2 == 0) or (gb == GROUPS - 1 and s == GT - 1):
                         final_add(nc.vector, gb, s)
                     else:
                         final_add(nc.gpsimd, gb, s)

@@ -26,8 +26,6 @@ TILES = ROWS // P
 GT = 4
 GROUPS = TILES // GT
 NB = C // P
-LAG_A = 2
-LAG_X = 3
 N_SPLIT = 10
 
 
@@ -109,11 +107,11 @@ def tile_tensormoe_pa_t_kernel(tc, x, W_im, W_in, leak_m, leak_n, out):
             nc.vector.tensor_copy(out=dst[:, :N_SPLIT], in_=src[:, :N_SPLIT])
             nc.scalar.copy(out=dst[:, N_SPLIT:], in_=src[:, N_SPLIT:])
 
-        def regroup_in(g):
-            nc.gpsimd.tensor_scalar(
-                out=grp_in[:, g].rearrange("p (n m) j -> p n m j", n=HN),
-                in0=raw_in[:, g].rearrange("p m (j n) -> p n m j", j=PACK),
-                scalar1=1.0, scalar2=0.0, op0=ALU.mult, op1=ALU.add,
+        def regroup_in(g, q):
+            ns = slice(q * 4, (q + 1) * 4)
+            nc.scalar.copy(
+                out=grp_in[:, g].rearrange("p (n m) j -> p n m j", n=HN)[:, ns],
+                in_=raw_in[:, g].rearrange("p m (j n) -> p n m j", j=PACK)[:, ns],
             )
 
         def quant_w(grp, wq, ws, g):
@@ -123,7 +121,8 @@ def tile_tensormoe_pa_t_kernel(tc, x, W_im, W_in, leak_m, leak_n, out):
                 in_=grp[:, g].rearrange("p c j -> p (c j)"),
             )
 
-        def transposes(gi, h):
+        def transposes(k):
+            gi, h = divmod(k, 2)
             for tt in (2 * h, 2 * h + 1):
                 xw = x_tiles[gi][:, tt, :].bitcast(F32)
                 xt = psx.tile([P, PACK, P], F32, name="xt")
@@ -134,7 +133,8 @@ def tile_tensormoe_pa_t_kernel(tc, x, W_im, W_in, leak_m, leak_n, out):
                         xt[:, q, :], xw[:, 256 * g + u : 256 * (g + 1) : 2], ident[:]
                     )
 
-        def evac(gi, h):
+        def evac(k):
+            gi, h = divmod(k, 2)
             gr = grpool.tile([P, 2, PASSES, P, 2], F32, name="gr", align_bytes=64)
             gr_tiles[(gi, h)] = gr
             for e in range(2):
@@ -143,7 +143,8 @@ def tile_tensormoe_pa_t_kernel(tc, x, W_im, W_in, leak_m, leak_n, out):
                     in_=xt_tiles[(gi, 2 * h + e)][:].rearrange("p (g u) b -> p g b u", u=2),
                 )
 
-        def quant_x(gi, h):
+        def quant_x(k):
+            gi, h = divmod(k, 2)
             t = gi * GT + 2 * h
             nc.vector.quantize_mx(
                 out=xq[:, t : t + 2, :].rearrange("p t w -> p (t w)").bitcast(FP8X4),
@@ -234,54 +235,72 @@ def tile_tensormoe_pa_t_kernel(tc, x, W_im, W_in, leak_m, leak_n, out):
             out=dn[:], in0=ln_bf[:], scalar1=-1.0, scalar2=1.0, op0=ALU.mult, op1=ALU.add,
         )
 
-        for gb in range(-LAG_X, GROUPS):
-            ga = gb + LAG_A
-            gx = gb + LAG_X
-            do_x = gx < GROUPS
+        def store_cols(gi, j):
+            cols = slice(j * P, (j + 1) * P)
+            nc.sync.dma_start(out=ov[:, gi * GT : (gi + 1) * GT, cols], in_=y2_tiles[gi][:, :, cols])
+
+        TA = 4
+        TB = TA + 9
+        late = []
+        first = (0, 2)
+        pair_at = {}
+        quant_at = {}
+        for k in range(2 * GROUPS):
+            tk = first[k] if k < len(first) else 2 * k
+            pair_at.setdefault(tk, []).append(k)
+            quant_at.setdefault(tk + 2, []).append(k)
+
+        for t in range(TB + 4 * GROUPS):
+            ga, sa = divmod(t - TA, GT)
+            gb, sb = divmod(t - TB, GT)
+            s = sb
             do_a = 0 <= ga < GROUPS
             do_b = gb >= 0
-            for s in range(GT):
-                if gx == 0 and s >= 2:
-                    regroup_im(s - 2)
-                if do_a:
-                    a_passes(ga, s)
-                if do_b:
-                    b_passes(gb, s)
-                if do_x and s % 2 == 0:
-                    transposes(gx, s // 2)
-                    if s == 2 and gx + 4 < GROUPS:
-                        load_x(gx + 4, 1)
-                if do_x and s % 2 == 1:
-                    evac(gx, s // 2)
-                if do_b:
-                    b_relu(gb, s)
-                if do_a:
-                    a_mul(ga, s)
-                if do_b:
-                    b_elem(gb, s, (0, 1, 2))
-                if do_x and s == 2:
-                    quant_x(gx, 0)
-                if 0 < gx <= GROUPS and s == 0:
-                    quant_x(gx - 1, 1)
-                if gx == 0 and s >= 2:
-                    quant_w(grp_im, wq_im, ws_im, s - 2)
-                if gx == 1 and s >= 2:
-                    regroup_in(s - 2)
-                if gx == 2 and s >= 2:
-                    quant_w(grp_in, wq_in, ws_in, s - 2)
-                if do_b:
-                    b_elem(gb, s, (3,))
-                if do_a:
-                    a_add(ga, s)
-                if do_b:
-                    if (not do_a and s % 2 == 0) or (gb == GROUPS - 1 and s == GT - 1):
-                        final_add(nc.vector, gb, s)
-                    else:
-                        final_add(nc.gpsimd, gb, s)
-                    if gb == GROUPS - 1:
-                        cols = slice(s * P, (s + 1) * P)
-                        nc.sync.dma_start(
-                            out=ov[:, gb * GT : (gb + 1) * GT, cols], in_=y2_tiles[gb][:, :, cols]
-                        )
-            if do_b and gb < GROUPS - 1:
-                nc.sync.dma_start(out=ov[:, gb * GT : (gb + 1) * GT, :], in_=y2_tiles[gb][:])
+            if 2 <= t < 4:
+                regroup_im(t - 2)
+            if do_a:
+                a_passes(ga, sa)
+            if do_b:
+                b_passes(gb, sb)
+            for k in pair_at.get(t, ()):
+                transposes(k)
+                if k % 2 == 1 and k // 2 + 4 < GROUPS:
+                    load_x(k // 2 + 4, 1)
+            for k in pair_at.get(t - 1, ()):
+                evac(k)
+            if do_b:
+                b_relu(gb, sb)
+            if 9 <= t < 13:
+                for i in range(2):
+                    regroup_in(*divmod((t - 9) * 2 + i, 4))
+            if do_a:
+                a_mul(ga, sa)
+            if do_b:
+                b_elem(gb, sb, (0, 1, 2))
+            for k in quant_at.get(t, ()):
+                quant_x(k)
+            if 2 <= t < 4:
+                quant_w(grp_im, wq_im, ws_im, t - 2)
+            if t in (11, 12):
+                quant_w(grp_in, wq_in, ws_in, t - 11)
+            if do_b:
+                b_elem(gb, sb, (3,))
+            if do_a:
+                a_add(ga, sa)
+            if do_b:
+                on_vector = not do_a and s % 2 == 0
+                if not on_vector and not (gb == GROUPS - 1 and sb == GT - 1):
+                    final_add(nc.gpsimd, gb, sb)
+                if late:
+                    final_add(nc.vector, *late[0])
+                    if late[0][0] == GROUPS - 1:
+                        store_cols(*late[0])
+                    late.clear()
+                if gb == GROUPS - 1 and sb == GT - 1:
+                    final_add(nc.vector, gb, sb)
+                elif on_vector:
+                    late.append((gb, sb))
+                if gb == GROUPS - 1 and not late:
+                    store_cols(gb, sb)
+            if do_b and sb == 0 and 0 < gb:
+                nc.sync.dma_start(out=ov[:, (gb - 1) * GT : gb * GT, :], in_=y2_tiles[gb - 1][:])

@@ -110,8 +110,8 @@ def tile_tensormoe_pa_t_kernel(tc, x, W_im, W_in, leak_m, leak_n, out):
         def regroup_in(g, q):
             ns = slice(q * 4, (q + 1) * 4)
             nc.scalar.copy(
-                out=grp_in[:, g].rearrange("p (n m) j -> p n m j", n=HN)[:, ns],
-                in_=raw_in[:, g].rearrange("p m (j n) -> p n m j", j=PACK)[:, ns],
+                out=grp_in[:, g].rearrange("p (n m) j -> p m j n", n=HN)[:, :, :, ns],
+                in_=raw_in[:, g].rearrange("p m (j n) -> p m j n", j=PACK)[:, :, :, ns],
             )
 
         def quant_w(grp, wq, ws, g):
@@ -270,9 +270,9 @@ def tile_tensormoe_pa_t_kernel(tc, x, W_im, W_in, leak_m, leak_n, out):
                 evac(k)
             if do_b:
                 b_relu(gb, sb)
-            if 9 <= t < 13:
+            if 8 <= t < 12:
                 for i in range(2):
-                    regroup_in(*divmod((t - 9) * 2 + i, 4))
+                    regroup_in(*divmod((t - 8) * 2 + i, 4))
             if do_a:
                 a_mul(ga, sa)
             if do_b:

@@ -102,8 +102,8 @@ def tile_tensormoe_pa_t_kernel(tc, x, W_im, W_in, leak_m, leak_n, out):
             )
 
         def regroup_im(g):
-            dst = grp_im[:, g].rearrange("p (n m) j -> p n m j", n=HN)
-            src = raw_im[:, g].rearrange("p n (j m) -> p n m j", j=PACK)
+            dst = grp_im[:, g].rearrange("p (n w q) j -> p n w j q", n=HN, q=PACK)
+            src = raw_im[:, g].rearrange("p n (j w q) -> p n w j q", j=PACK, q=PACK)
             nc.vector.tensor_copy(out=dst[:, :N_SPLIT], in_=src[:, :N_SPLIT])
             nc.scalar.copy(out=dst[:, N_SPLIT:], in_=src[:, N_SPLIT:])
 
@@ -235,12 +235,12 @@ def tile_tensormoe_pa_t_kernel(tc, x, W_im, W_in, leak_m, leak_n, out):
             out=dn[:], in0=ln_bf[:], scalar1=-1.0, scalar2=1.0, op0=ALU.mult, op1=ALU.add,
         )
 
-        def store_cols(gi, j):
-            cols = slice(j * P, (j + 1) * P)
+        def store_pair(gi, j):
+            cols = slice((j - 1) * P, (j + 1) * P)
             nc.sync.dma_start(out=ov[:, gi * GT : (gi + 1) * GT, cols], in_=y2_tiles[gi][:, :, cols])
 
         TA = 4
-        TB = TA + 9
+        TB = TA + 8
         late = []
         first = (0, 2)
         pair_at = {}
@@ -253,7 +253,6 @@ def tile_tensormoe_pa_t_kernel(tc, x, W_im, W_in, leak_m, leak_n, out):
         for t in range(TB + 4 * GROUPS):
             ga, sa = divmod(t - TA, GT)
             gb, sb = divmod(t - TB, GT)
-            s = sb
             do_a = 0 <= ga < GROUPS
             do_b = gb >= 0
             if 2 <= t < 4:
@@ -270,9 +269,9 @@ def tile_tensormoe_pa_t_kernel(tc, x, W_im, W_in, leak_m, leak_n, out):
                 evac(k)
             if do_b:
                 b_relu(gb, sb)
-            if 8 <= t < 12:
+            if 7 <= t < 11:
                 for i in range(2):
-                    regroup_in(*divmod((t - 8) * 2 + i, 4))
+                    regroup_in(*divmod((t - 7) * 2 + i, 4))
             if do_a:
                 a_mul(ga, sa)
             if do_b:
@@ -281,26 +280,25 @@ def tile_tensormoe_pa_t_kernel(tc, x, W_im, W_in, leak_m, leak_n, out):
                 quant_x(k)
             if 2 <= t < 4:
                 quant_w(grp_im, wq_im, ws_im, t - 2)
-            if t in (11, 12):
-                quant_w(grp_in, wq_in, ws_in, t - 11)
+            if t in (10, 11):
+                quant_w(grp_in, wq_in, ws_in, t - 10)
             if do_b:
                 b_elem(gb, sb, (3,))
             if do_a:
                 a_add(ga, sa)
             if do_b:
-                on_vector = not do_a and s % 2 == 0
-                if not on_vector and not (gb == GROUPS - 1 and sb == GT - 1):
+                on_vector = not do_a and sb % 2 == 1
+                last = gb == GROUPS - 1 and sb == GT - 1
+                if not on_vector:
                     final_add(nc.gpsimd, gb, sb)
-                if late:
-                    final_add(nc.vector, *late[0])
-                    if late[0][0] == GROUPS - 1:
-                        store_cols(*late[0])
-                    late.clear()
-                if gb == GROUPS - 1 and sb == GT - 1:
-                    final_add(nc.vector, gb, sb)
-                elif on_vector:
+                    if sb % 2 == 1:
+                        store_pair(gb, sb)
+                elif not last:
                     late.append((gb, sb))
-                if gb == GROUPS - 1 and not late:
-                    store_cols(gb, sb)
-            if do_b and sb == 0 and 0 < gb:
-                nc.sync.dma_start(out=ov[:, (gb - 1) * GT : gb * GT, :], in_=y2_tiles[gb - 1][:])
+                if late and late[0] != (gb, sb):
+                    final_add(nc.vector, *late[0])
+                    store_pair(*late[0])
+                    late.clear()
+                if last:
+                    final_add(nc.vector, gb, sb)
+                    store_pair(gb, sb)

@@ -76,11 +76,13 @@ def tile_tensormoe_pa_t_kernel(tc, x, W_im, W_in, leak_m, leak_n, out):
         y1_tiles = {}
         y2_tiles = {}
 
-        def load_w_im(g):
-            nc.sync.dma_start(
-                out=raw_im[:, g],
-                in_=W_im[:, g * K_PASS : (g + 1) * K_PASS, :].rearrange("n (p j) m -> p n (j m)", j=PACK),
-            )
+        def load_w_im(h):
+            ns = slice(h * HN // 2, (h + 1) * HN // 2)
+            for g in range(PASSES):
+                nc.sync.dma_start(
+                    out=raw_im[:, g, ns],
+                    in_=W_im[ns, g * K_PASS : (g + 1) * K_PASS, :].rearrange("n (p j) m -> p n (j m)", j=PACK),
+                )
 
         def load_x(gi, pieces):
             x_sb = xpool.tile([P, GT, K], BF16, name="x_sb")
@@ -91,9 +93,8 @@ def tile_tensormoe_pa_t_kernel(tc, x, W_im, W_in, leak_m, leak_n, out):
                     out=x_sb[:, h * step : (h + 1) * step, :],
                     in_=xv[:, gi * GT + h * step : gi * GT + (h + 1) * step, :],
                 )
-                if gi == 0 and h == 0:
-                    load_w_im(0)
-                    load_w_im(1)
+                if gi == 0:
+                    load_w_im(h)
 
         def load_w_in(g):
             nc.sync.dma_start(
@@ -101,11 +102,22 @@ def tile_tensormoe_pa_t_kernel(tc, x, W_im, W_in, leak_m, leak_n, out):
                 in_=W_in[:, g * K_PASS : (g + 1) * K_PASS, :].rearrange("m (p j) n -> p m (j n)", j=PACK),
             )
 
-        def regroup_im(g):
-            dst = grp_im[:, g].rearrange("p (n w q) j -> p n w j q", n=HN, q=PACK)
-            src = raw_im[:, g].rearrange("p n (j w q) -> p n w j q", j=PACK, q=PACK)
-            nc.vector.tensor_copy(out=dst[:, :N_SPLIT], in_=src[:, :N_SPLIT])
-            nc.scalar.copy(out=dst[:, N_SPLIT:], in_=src[:, N_SPLIT:])
+        def regroup_im(h):
+            for g in range(PASSES):
+                lo, mid, hi = h * HN // 2, h * HN // 2 + 5, (h + 1) * HN // 2
+                dst = grp_im[:, g].rearrange("p (n w q) j -> p n w j q", n=HN, q=PACK)
+                src = raw_im[:, g].rearrange("p n (j w q) -> p n w j q", j=PACK, q=PACK)
+                nc.vector.tensor_copy(out=dst[:, lo:mid], in_=src[:, lo:mid])
+                nc.scalar.copy(out=dst[:, mid:hi], in_=src[:, mid:hi])
+
+        def quant_im(h):
+            cols = slice(h * C // 2, (h + 1) * C // 2)
+            for g in range(PASSES):
+                nc.vector.quantize_mx(
+                    out=wq_im[:, g, cols].bitcast(FP8X4),
+                    scales=ws_im[:, g, cols],
+                    in_=grp_im[:, g, cols].rearrange("p c j -> p (c j)"),
+                )
 
         def regroup_in(g, q):
             ns = slice(q * 4, (q + 1) * 4)
@@ -161,6 +173,31 @@ def tile_tensormoe_pa_t_kernel(tc, x, W_im, W_in, leak_m, leak_n, out):
                 rhs_scale=ws[:, g, cols],
                 start=(g == 0),
                 stop=(g == PASSES - 1),
+            )
+
+        def a_half(tt, h):
+            if h == 0:
+                a_tiles[(0, tt)] = psa.tile([P, C], F32, name="a_ps")
+            cols = slice(h * C // 2, (h + 1) * C // 2)
+            for g in range(PASSES):
+                mx(a_tiles[(0, tt)][:, cols], tt, g, wq_im, ws_im, cols)
+
+        def a_mul_half(tt, h):
+            if h == 0:
+                t1_tiles[(0, tt)] = work.tile([P, C], F32, name="t1")
+            cols = slice(h * C // 2, (h + 1) * C // 2)
+            nc.vector.scalar_tensor_tensor(
+                out=t1_tiles[(0, tt)][:, cols], in0=a_tiles[(0, tt)][:, cols], scalar=0.0,
+                in1=lm1[:].rearrange("p n m -> p (n m)")[:, cols], op0=ALU.min, op1=ALU.mult,
+            )
+
+        def a_add_half(tt, h):
+            if tt == 0 and h == 0:
+                y1_tiles[0] = y1pool.tile([P, GT, C], F32, name="y1")
+            cols = slice(h * C // 2, (h + 1) * C // 2)
+            nc.vector.tensor_tensor(
+                out=y1_tiles[0][:, tt, cols], in0=a_tiles[(0, tt)][:, cols],
+                in1=t1_tiles[(0, tt)][:, cols], op=ALU.add,
             )
 
         def a_passes(gi, tt):
@@ -221,7 +258,7 @@ def tile_tensormoe_pa_t_kernel(tc, x, W_im, W_in, leak_m, leak_n, out):
             )
 
         load_x(0, 2)
-        load_x(1, 1)
+        load_x(1, 2)
         load_x(2, 1)
         load_w_in(0)
         load_w_in(1)
@@ -257,7 +294,10 @@ def tile_tensormoe_pa_t_kernel(tc, x, W_im, W_in, leak_m, leak_n, out):
             do_b = gb >= 0
             if 2 <= t < 4:
                 regroup_im(t - 2)
-            if do_a:
+            if do_a and ga == 0 and sa < 2:
+                a_half(0, sa)
+                a_half(1, sa)
+            elif do_a:
                 a_passes(ga, sa)
             if do_b:
                 b_passes(gb, sb)
@@ -272,33 +312,44 @@ def tile_tensormoe_pa_t_kernel(tc, x, W_im, W_in, leak_m, leak_n, out):
             if 7 <= t < 11:
                 for i in range(2):
                     regroup_in(*divmod((t - 7) * 2 + i, 4))
-            if do_a:
+            if do_a and ga == 0 and sa < 2:
+                if sa == 0:
+                    a_mul_half(0, 0)
+                    a_mul_half(1, 0)
+                    a_add_half(0, 0)
+                    a_add_half(1, 0)
+                else:
+                    a_mul_half(0, 1)
+                    a_mul_half(1, 1)
+                    a_add_half(0, 1)
+                    a_add_half(1, 1)
+            elif do_a:
                 a_mul(ga, sa)
             if do_b:
                 b_elem(gb, sb, (0, 1, 2))
             for k in quant_at.get(t, ()):
                 quant_x(k)
             if 2 <= t < 4:
-                quant_w(grp_im, wq_im, ws_im, t - 2)
+                quant_im(t - 2)
             if t in (10, 11):
                 quant_w(grp_in, wq_in, ws_in, t - 10)
             if do_b:
                 b_elem(gb, sb, (3,))
-            if do_a:
+            if do_a and not (ga == 0 and sa < 2):
                 a_add(ga, sa)
             if do_b:
-                on_vector = not do_a and sb % 2 == 1
                 last = gb == GROUPS - 1 and sb == GT - 1
+                on_vector = not do_a and (sb % 2 == 1 or last)
                 if not on_vector:
                     final_add(nc.gpsimd, gb, sb)
-                    if sb % 2 == 1:
-                        store_pair(gb, sb)
-                elif not last:
-                    late.append((gb, sb))
-                if late and late[0] != (gb, sb):
+                if late:
                     final_add(nc.vector, *late[0])
-                    store_pair(*late[0])
+                    if late[0][1] % 2 == 1:
+                        store_pair(*late[0])
                     late.clear()
                 if last:
                     final_add(nc.vector, gb, sb)
+                elif on_vector:
+                    late.append((gb, sb))
+                if sb % 2 == 1 and (last or not on_vector):
                     store_pair(gb, sb)

@@ -104,7 +104,7 @@ def tile_tensormoe_pa_t_kernel(tc, x, W_im, W_in, leak_m, leak_n, out):
 
         def regroup_im(h):
             for g in range(PASSES):
-                lo, mid, hi = h * HN // 2, h * HN // 2 + 5, (h + 1) * HN // 2
+                lo, mid, hi = h * HN // 2, h * HN // 2 + 6, (h + 1) * HN // 2
                 dst = grp_im[:, g].rearrange("p (n w q) j -> p n w j q", n=HN, q=PACK)
                 src = raw_im[:, g].rearrange("p n (j w q) -> p n w j q", j=PACK, q=PACK)
                 nc.vector.tensor_copy(out=dst[:, lo:mid], in_=src[:, lo:mid])
@@ -259,8 +259,8 @@ def tile_tensormoe_pa_t_kernel(tc, x, W_im, W_in, leak_m, leak_n, out):
 
         load_x(0, 2)
         load_x(1, 2)
-        load_x(2, 1)
         load_w_in(0)
+        load_x(2, 1)
         load_w_in(1)
         load_x(3, 1)
 
@@ -325,21 +325,24 @@ def tile_tensormoe_pa_t_kernel(tc, x, W_im, W_in, leak_m, leak_n, out):
                     a_add_half(1, 1)
             elif do_a:
                 a_mul(ga, sa)
+            pa, qa = divmod(t - TA - 1, GT)
+            if 0 <= pa < GROUPS and t - 1 < TB and not (pa == 0 and qa < 2):
+                a_add(pa, qa)
             if do_b:
                 b_elem(gb, sb, (0, 1, 2))
             for k in quant_at.get(t, ()):
                 quant_x(k)
             if 2 <= t < 4:
                 quant_im(t - 2)
-            if t in (10, 11):
-                quant_w(grp_in, wq_in, ws_in, t - 10)
+            if t in (9, 10):
+                quant_w(grp_in, wq_in, ws_in, t - 9)
             if do_b:
                 b_elem(gb, sb, (3,))
-            if do_a and not (ga == 0 and sa < 2):
+            if do_a and t >= TB and not (ga == 0 and sa < 2):
                 a_add(ga, sa)
             if do_b:
                 last = gb == GROUPS - 1 and sb == GT - 1
-                on_vector = not do_a and (sb % 2 == 1 or last)
+                on_vector = not do_a and (t % 3 == 1 or last)
                 if not on_vector:
                     final_add(nc.gpsimd, gb, sb)
                 if late:

from contextlib import ExitStack

import concourse.mybir as mybir
from concourse.masks import make_identity

FLOPS = 2 * 4096 * 1024 * 1024

F32 = mybir.dt.float32
BF16 = mybir.dt.bfloat16
U32 = mybir.dt.uint32
U8 = mybir.dt.uint8
FP8X4 = mybir.dt.float8_e4m3fn_x4
ALU = mybir.AluOpType
ACT = mybir.ActivationFunctionType

P = 128
ROWS = 4096
K = 1024
HN = 16
HM = 32
C = HN * HM
PACK = 4
K_PASS = P * PACK
PASSES = K // K_PASS
TILES = ROWS // P
GT = 4
GROUPS = TILES // GT
NB = C // P
N_SPLIT = 10


def tile_tensormoe_pa_t_kernel(tc, x, W_im, W_in, leak_m, leak_n, out):
    nc = tc.nc
    xv = x.rearrange("(p t) k -> p t k", t=TILES)
    ov = out.rearrange("(p t) n m -> p t (n m)", t=TILES)

    with ExitStack() as ctx:
        const = ctx.enter_context(tc.tile_pool(name="const", bufs=1))
        xpool = ctx.enter_context(tc.tile_pool(name="xpool", bufs=4))
        grpool = ctx.enter_context(tc.tile_pool(name="grpool", bufs=3))
        work = ctx.enter_context(tc.tile_pool(name="work", bufs=3))
        y1pool = ctx.enter_context(tc.tile_pool(name="y1pool", bufs=4))
        y2pool = ctx.enter_context(tc.tile_pool(name="y2pool", bufs=3))
        psx = ctx.enter_context(tc.psum_pool(name="psx", bufs=2))
        psa = ctx.enter_context(tc.psum_pool(name="psa", bufs=3))
        psb = ctx.enter_context(tc.psum_pool(name="psb", bufs=3))
        ctx.enter_context(tc.manual_schedule())

        ident = const.tile([P, P], F32, name="ident")
        make_identity(nc, ident[:])
        lm_bf = const.tile([P, HM], BF16, name="lm_bf")
        ln_bf = const.tile([P, HN], BF16, name="ln_bf")
        nc.scalar.dma_start(out=lm_bf[:], in_=leak_m.partition_broadcast(P))
        nc.scalar.dma_start(out=ln_bf[:], in_=leak_n.partition_broadcast(P))

        xq = const.tile([P, TILES, PASSES * P], U32, name="xq", align_bytes=64)
        xs = const.tile([P, TILES, PASSES * P], U8, name="xs", align_bytes=64)
        raw_im = const.tile([P, PASSES, HN, PACK * HM], BF16, name="raw_im")
        raw_in = const.tile([P, PASSES, HM, PACK * HN], BF16, name="raw_in")
        grp_im = const.tile([P, PASSES, C, PACK], BF16, name="grp_im", align_bytes=64)
        grp_in = const.tile([P, PASSES, C, PACK], BF16, name="grp_in", align_bytes=64)
        wq_im = const.tile([P, PASSES, C], U32, name="wq_im", align_bytes=64)
        wq_in = const.tile([P, PASSES, C], U32, name="wq_in", align_bytes=64)
        ws_im = const.tile([P, PASSES, C], U8, name="ws_im", align_bytes=64)
        ws_in = const.tile([P, PASSES, C], U8, name="ws_in", align_bytes=64)
        lm1 = const.tile([P, HN, HM], F32, name="lm1")
        dn = const.tile([P, HN], F32, name="dn")

        x_tiles = {}
        xt_tiles = {}
        gr_tiles = {}
        a_tiles = {}
        t1_tiles = {}
        b_tiles = {}
        rb_tiles = {}
        y1_tiles = {}
        y2_tiles = {}

        def load_w_im(h):
            ns = slice(h * HN // 2, (h + 1) * HN // 2)
            for g in range(PASSES):
                nc.sync.dma_start(
                    out=raw_im[:, g, ns],
                    in_=W_im[ns, g * K_PASS : (g + 1) * K_PASS, :].rearrange("n (p j) m -> p n (j m)", j=PACK),
                )

        def load_x(gi, pieces):
            x_sb = xpool.tile([P, GT, K], BF16, name="x_sb")
            x_tiles[gi] = x_sb
            step = GT // pieces
            for h in range(pieces):
                nc.sync.dma_start(
                    out=x_sb[:, h * step : (h + 1) * step, :],
                    in_=xv[:, gi * GT + h * step : gi * GT + (h + 1) * step, :],
                )
                if gi == 0:
                    load_w_im(h)

        def load_w_in(g):
            nc.sync.dma_start(
                out=raw_in[:, g],
                in_=W_in[:, g * K_PASS : (g + 1) * K_PASS, :].rearrange("m (p j) n -> p m (j n)", j=PACK),
            )

        def regroup_im(h):
            for g in range(PASSES):
                lo, mid, hi = h * HN // 2, h * HN // 2 + 6, (h + 1) * HN // 2
                dst = grp_im[:, g].rearrange("p (n w q) j -> p n w j q", n=HN, q=PACK)
                src = raw_im[:, g].rearrange("p n (j w q) -> p n w j q", j=PACK, q=PACK)
                nc.vector.tensor_copy(out=dst[:, lo:mid], in_=src[:, lo:mid])
                nc.scalar.copy(out=dst[:, mid:hi], in_=src[:, mid:hi])

        def quant_im(h):
            cols = slice(h * C // 2, (h + 1) * C // 2)
            for g in range(PASSES):
                nc.vector.quantize_mx(
                    out=wq_im[:, g, cols].bitcast(FP8X4),
                    scales=ws_im[:, g, cols],
                    in_=grp_im[:, g, cols].rearrange("p c j -> p (c j)"),
                )

        def regroup_in(g, q):
            ns = slice(q * 4, (q + 1) * 4)
            nc.scalar.copy(
                out=grp_in[:, g].rearrange("p (n m) j -> p m j n", n=HN)[:, :, :, ns],
                in_=raw_in[:, g].rearrange("p m (j n) -> p m j n", j=PACK)[:, :, :, ns],
            )

        def quant_w(grp, wq, ws, g):
            nc.vector.quantize_mx(
                out=wq[:, g, :].bitcast(FP8X4),
                scales=ws[:, g, :],
                in_=grp[:, g].rearrange("p c j -> p (c j)"),
            )

        def transposes(k):
            gi, h = divmod(k, 2)
            for tt in (2 * h, 2 * h + 1):
                xw = x_tiles[gi][:, tt, :].bitcast(F32)
                xt = psx.tile([P, PACK, P], F32, name="xt")
                xt_tiles[(gi, tt)] = xt
                for q in range(PACK):
                    g, u = divmod(q, 2)
                    nc.tensor.transpose(
                        xt[:, q, :], xw[:, 256 * g + u : 256 * (g + 1) : 2], ident[:]
                    )

        def evac(k):
            gi, h = divmod(k, 2)
            gr = grpool.tile([P, 2, PASSES, P, 2], F32, name="gr", align_bytes=64)
            gr_tiles[(gi, h)] = gr
            for e in range(2):
                nc.scalar.copy(
                    out=gr[:, e],
                    in_=xt_tiles[(gi, 2 * h + e)][:].rearrange("p (g u) b -> p g b u", u=2),
                )

        def quant_x(k):
            gi, h = divmod(k, 2)
            t = gi * GT + 2 * h
            nc.vector.quantize_mx(
                out=xq[:, t : t + 2, :].rearrange("p t w -> p (t w)").bitcast(FP8X4),
                scales=xs[:, t : t + 2, :].rearrange("p t w -> p (t w)"),
                in_=gr_tiles[(gi, h)][:].rearrange("p e g b u -> p (e g b u)").bitcast(BF16),
            )

        def mx(acc, t, g, wq, ws, cols):
            nc.tensor.matmul_mx(
                out=acc,
                lhsT=xq[:, t, g * P : (g + 1) * P].bitcast(FP8X4),
                lhsT_scale=xs[:, t, g * P : (g + 1) * P],
                rhs=wq[:, g, cols].bitcast(FP8X4),
                rhs_scale=ws[:, g, cols],
                start=(g == 0),
                stop=(g == PASSES - 1),
            )

        def a_half(tt, h):
            if h == 0:
                a_tiles[(0, tt)] = psa.tile([P, C], F32, name="a_ps")
            cols = slice(h * C // 2, (h + 1) * C // 2)
            for g in range(PASSES):
                mx(a_tiles[(0, tt)][:, cols], tt, g, wq_im, ws_im, cols)

        def a_mul_half(tt, h):
            if h == 0:
                t1_tiles[(0, tt)] = work.tile([P, C], F32, name="t1")
            cols = slice(h * C // 2, (h + 1) * C // 2)
            nc.vector.scalar_tensor_tensor(
                out=t1_tiles[(0, tt)][:, cols], in0=a_tiles[(0, tt)][:, cols], scalar=0.0,
                in1=lm1[:].rearrange("p n m -> p (n m)")[:, cols], op0=ALU.min, op1=ALU.mult,
            )

        def a_add_half(tt, h):
            if tt == 0 and h == 0:
                y1_tiles[0] = y1pool.tile([P, GT, C], F32, name="y1")
            cols = slice(h * C // 2, (h + 1) * C // 2)
            nc.vector.tensor_tensor(
                out=y1_tiles[0][:, tt, cols], in0=a_tiles[(0, tt)][:, cols],
                in1=t1_tiles[(0, tt)][:, cols], op=ALU.add,
            )

        def a_passes(gi, tt):
            a_ps = psa.tile([P, C], F32, name="a_ps")
            a_tiles[(gi, tt)] = a_ps
            for g in range(PASSES):
                mx(a_ps[:], gi * GT + tt, g, wq_im, ws_im, slice(0, C))

        def b_passes(gi, j):
            b_ps = psb.tile([P, GT, P], F32, name="b_ps")
            b_tiles[(gi, j)] = b_ps
            for tt in range(GT):
                for g in range(PASSES):
                    mx(b_ps[:, tt, :], gi * GT + tt, g, wq_in, ws_in, slice(j * P, (j + 1) * P))

        def a_mul(gi, tt):
            t1 = work.tile([P, C], F32, name="t1")
            t1_tiles[(gi, tt)] = t1
            nc.vector.scalar_tensor_tensor(
                out=t1[:], in0=a_tiles[(gi, tt)][:], scalar=0.0,
                in1=lm1[:].rearrange("p n m -> p (n m)"), op0=ALU.min, op1=ALU.mult,
            )

        def a_add(gi, tt):
            if tt == 0:
                y1 = y1pool.tile([P, GT, C], F32, name="y1")
                y1_tiles[gi] = y1
            nc.vector.tensor_tensor(
                out=y1_tiles[gi][:, tt, :], in0=a_tiles[(gi, tt)][:], in1=t1_tiles[(gi, tt)][:],
                op=ALU.add,
            )

        def b_relu(gi, j):
            rb = work.tile([P, GT, P], F32, name="rb")
            rb_tiles[(gi, j)] = rb
            nc.scalar.activation(out=rb[:], in_=b_tiles[(gi, j)][:], func=ACT.Relu, scale=-1.0)

        def b_elem(gi, j, slices):
            if j == 0 and slices[0] == 0:
                y2 = y2pool.tile([P, GT, C], F32, name="y2")
                y2_tiles[gi] = y2
            y2 = y2_tiles[gi]
            for nl in slices:
                n = j * (P // HM) + nl
                nc.vector.scalar_tensor_tensor(
                    out=y2[:, :, n * HM : (n + 1) * HM],
                    in0=rb_tiles[(gi, j)][:, :, nl * HM : (nl + 1) * HM],
                    scalar=dn[:, n : n + 1],
                    in1=b_tiles[(gi, j)][:, :, nl * HM : (nl + 1) * HM],
                    op0=ALU.mult, op1=ALU.add,
                )

        def final_add(eng, gi, j):
            cols = slice(j * P, (j + 1) * P)
            eng.tensor_tensor(
                out=y2_tiles[gi][:, :, cols], in0=y1_tiles[gi][:, :, cols],
                in1=y2_tiles[gi][:, :, cols], op=ALU.add,
            )

        load_x(0, 2)
        load_x(1, 2)
        load_w_in(0)
        load_x(2, 1)
        load_w_in(1)
        load_x(3, 1)

        nc.vector.tensor_scalar(
            out=lm1[:], in0=lm_bf[:].unsqueeze(1).to_broadcast([P, HN, HM]),
            scalar1=-1.0, scalar2=None, op0=ALU.add,
        )
        nc.vector.tensor_scalar(
            out=dn[:], in0=ln_bf[:], scalar1=-1.0, scalar2=1.0, op0=ALU.mult, op1=ALU.add,
        )

        def store_pair(gi, j):
            cols = slice((j - 1) * P, (j + 1) * P)
            nc.sync.dma_start(out=ov[:, gi * GT : (gi + 1) * GT, cols], in_=y2_tiles[gi][:, :, cols])

        TA = 4
        TB = TA + 8
        late = []
        first = (0, 2)
        pair_at = {}
        quant_at = {}
        for k in range(2 * GROUPS):
            tk = first[k] if k < len(first) else 2 * k
            pair_at.setdefault(tk, []).append(k)
            quant_at.setdefault(tk + 2, []).append(k)

        for t in range(TB + 4 * GROUPS):
            ga, sa = divmod(t - TA, GT)
            gb, sb = divmod(t - TB, GT)
            do_a = 0 <= ga < GROUPS
            do_b = gb >= 0
            if 2 <= t < 4:
                regroup_im(t - 2)
            if do_a and ga == 0 and sa < 2:
                a_half(0, sa)
                a_half(1, sa)
            elif do_a:
                a_passes(ga, sa)
            if do_b:
                b_passes(gb, sb)
            for k in pair_at.get(t, ()):
                transposes(k)
                if k % 2 == 1 and k // 2 + 4 < GROUPS:
                    load_x(k // 2 + 4, 1)
            for k in pair_at.get(t - 1, ()):
                evac(k)
            if do_b:
                b_relu(gb, sb)
            if 7 <= t < 11:
                for i in range(2):
                    regroup_in(*divmod((t - 7) * 2 + i, 4))
            if do_a and ga == 0 and sa < 2:
                if sa == 0:
                    a_mul_half(0, 0)
                    a_mul_half(1, 0)
                    a_add_half(0, 0)
                    a_add_half(1, 0)
                else:
                    a_mul_half(0, 1)
                    a_mul_half(1, 1)
                    a_add_half(0, 1)
                    a_add_half(1, 1)
            elif do_a:
                a_mul(ga, sa)
            pa, qa = divmod(t - TA - 1, GT)
            if 0 <= pa < GROUPS and t - 1 < TB and not (pa == 0 and qa < 2):
                a_add(pa, qa)
            if do_b:
                b_elem(gb, sb, (0, 1, 2))
            for k in quant_at.get(t, ()):
                quant_x(k)
            if 2 <= t < 4:
                quant_im(t - 2)
            if t in (9, 10):
                quant_w(grp_in, wq_in, ws_in, t - 9)
            if do_b:
                b_elem(gb, sb, (3,))
            if do_a and t >= TB and not (ga == 0 and sa < 2):
                a_add(ga, sa)
            if do_b:
                last = gb == GROUPS - 1 and sb == GT - 1
                on_vector = not do_a and (t % 3 == 1 or last)
                if not on_vector:
                    final_add(nc.gpsimd, gb, sb)
                if late:
                    final_add(nc.vector, *late[0])
                    if late[0][1] % 2 == 1:
                        store_pair(*late[0])
                    late.clear()
                if last:
                    final_add(nc.vector, gb, sb)
                elif on_vector:
                    late.append((gb, sb))
                if sb % 2 == 1 and (last or not on_vector):
                    store_pair(gb, sb)
